import numpy as np
import ml_dtypes


def mxq(x, axis, fmt="e4m3"):
    dtype, down = {"e4m3": (ml_dtypes.float8_e4m3fn, 7), "e5m2": (ml_dtypes.float8_e5m2, 14)}[fmt]
    v = np.moveaxis(np.asarray(x, np.float32).astype(ml_dtypes.bfloat16).astype(np.float64), axis, -1)
    blocks = v.reshape(v.shape[:-1] + (-1, 32))
    amax = np.abs(blocks).max(-1, keepdims=True)
    byte = np.maximum(np.where(amax > 0, np.frexp(amax)[1] - 1 + 127, 0) - down, 1)
    scale = np.exp2(byte - 127.0)
    codes = (blocks / scale).astype(np.float32).astype(dtype).astype(np.float64)
    return np.moveaxis((codes * scale).reshape(v.shape), -1, axis)


WIDE = False


def mx_kscale(k):
    if not WIDE:
        return np.ones(k)
    levels = np.array([20, -20, 10, -10, 0])
    a = np.random.permutation(np.resize(levels, k // 512 * 4)).reshape(k // 512, 4)
    idx = np.arange(k)
    return np.exp2(a[idx // 512, idx % 128 // 32])


BF16 = ml_dtypes.bfloat16


def bf(x):
    return np.asarray(x, np.float32).astype(BF16)


def f64(x):
    return np.asarray(x).astype(np.float64)


M, K, N = 4096, 1024, 512
GS = 8.0


def binarize(v):
    return np.sign(np.clip(v, -1.0, 1.0))


def setup_inputs():
    s = mx_kscale(N)
    keep = (s <= s.min() * 4.0).astype(np.float64)
    x = np.random.standard_normal((M, K))
    w = np.random.standard_normal((K, N)) / np.sqrt(K) * keep[None, :]
    gamma = -(1.0 + 0.1 * np.random.standard_normal(1)) / np.sqrt(K) * np.sqrt(N / keep.sum())
    g = np.random.standard_normal((M, N)) * np.exp2(np.random.randint(-12, 1, (M, 1))) * GS * (s / s.min())[None, :]
    return {"x": bf(x), "w": bf(w), "gamma": bf(gamma), "grad_out": bf(g)}


def reference(x, w, gamma, grad_out):
    wb = np.abs(f64(gamma)) * binarize(f64(w))
    return mxq(f64(grad_out), 1, "e5m2") @ mxq(wb, 1, "e4m3").T

@@ -1,0 +1,193 @@
+from contextlib import ExitStack
+
+import concourse.mybir as mybir
+from concourse.masks import make_identity
+
+F32 = mybir.dt.float32
+BF16 = mybir.dt.bfloat16
+U32 = mybir.dt.uint32
+U8 = mybir.dt.uint8
+E4M3X4 = mybir.dt.float8_e4m3fn_x4
+E5M2X4 = mybir.dt.float8_e5m2_x4
+ACT = mybir.ActivationFunctionType
+ALU = mybir.AluOpType
+
+P = 128
+M, K, N = 4096, 1024, 512
+MT = M // P
+PAIRS = MT // 2
+FLOPS = 2 * M * K * N
+BYTES = K * N * 2 + 2 + M * N * 2 + M * K * 4
+
+G_CHUNKS = [2, 2, 4, 8, 8, 8]
+STORES = [2, 2, 4, 4, 4, 4, 4, 4, 4]
+
+
+def tile_binary_dense_t_kernel(tc, x, w, gamma, grad_out, out):
+    nc = tc.nc
+    with ExitStack() as ctx:
+        keep = ctx.enter_context(tc.tile_pool(name="keep", bufs=1))
+        ring = ctx.enter_context(tc.tile_pool(name="ring", bufs=3))
+        psum = ctx.enter_context(tc.psum_pool(name="psum", bufs=8))
+        ctx.enter_context(tc.manual_schedule())
+
+        gam = keep.tile([P, 1], BF16, name="gam")
+        nc.scalar.dma_start(out=gam[:], in_=gamma.partition_broadcast(P))
+
+        w_view = w.rearrange("(i p) n -> p i n", p=P)
+        w_raw = []
+        for h in range(2):
+            wr = keep.tile([P, 4 * N], BF16, name="w_raw%d" % h)
+            nc.sync.dma_start(
+                out=wr[:].rearrange("p (i n) -> p i n", i=4),
+                in_=w_view[:, 4 * h : 4 * h + 4, :],
+            )
+            w_raw.append(wr)
+
+        g_view = grad_out.rearrange("(p t) n -> p (t n)", t=MT)
+        g_words = {}
+        t0 = 0
+        for c, width in enumerate(G_CHUNKS):
+            gr = keep.tile([P, width * N], BF16, name="g_raw%d" % c)
+            nc.sync.dma_start(out=gr[:], in_=g_view[:, t0 * N : (t0 + width) * N])
+            gw = gr[:].bitcast(F32)
+            for a in range(width):
+                g_words[t0 + a] = gw[:, a * 256 : (a + 1) * 256]
+            t0 += width
+
+        ident = keep.tile([P, P], F32, name="ident")
+        make_identity(nc, ident[:])
+
+        gabs = keep.tile([P, 1], F32, name="gabs")
+        nc.scalar.activation(out=gabs[:], in_=gam[:], func=ACT.Abs)
+
+        wg = keep.tile([P, 4 * K], BF16, name="wg", align_bytes=64)
+        w_codes = keep.tile([P, K], U32, name="w_codes", align_bytes=64)
+        w_scales = keep.tile([P, K], U8, name="w_scales", align_bytes=64)
+        g_codes = keep.tile([P, M], U32, name="g_codes", align_bytes=64)
+        g_scales = keep.tile([P, M], U8, name="g_scales", align_bytes=64)
+
+        o_tiles = {}
+        store_of = {}
+        t0 = 0
+        for s, width in enumerate(STORES):
+            ot = keep.tile([P, width * K], F32, name="o%d" % s)
+            for a in range(width):
+                o_tiles[t0 + a] = ot[:, a * K : (a + 1) * K]
+            store_of[t0 + width - 1] = (ot, t0, width)
+            t0 += width
+        out_view = out.rearrange("(p t) k -> p (t k)", t=MT)
+
+        def transposes(words_a, words_b, name):
+            bank = psum.tile([P, 512], F32, name=name, tag="bank")
+            for a, words in enumerate((words_a, words_b)):
+                for u in range(2):
+                    nc.tensor.transpose(
+                        bank[:, u * 256 + a * P : u * 256 + (a + 1) * P],
+                        words[:, u * P : (u + 1) * P],
+                        ident[:],
+                    )
+            return bank
+
+        w_banks = []
+        for h in range(2):
+            ww = w_raw[h][:].bitcast(F32)
+            for b in range(2):
+                w_banks.append(
+                    transposes(
+                        ww[:, (2 * b) * 256 : (2 * b + 1) * 256],
+                        ww[:, (2 * b + 1) * 256 : (2 * b + 2) * 256],
+                        "wt%d%d" % (h, b),
+                    )
+                )
+
+        def w_sign_mult(q):
+            sg = ring.tile([P, 1024], BF16, name="sg%d" % q, tag="sg")
+            nc.scalar.activation(
+                out=sg[:].rearrange("p (k u e) -> p k u e", u=2, e=2),
+                in_=w_banks[q][:].bitcast(BF16).rearrange("p (u k e) -> p k u e", u=2, e=2),
+                func=ACT.Sign,
+            )
+            nc.vector.tensor_scalar(
+                out=wg[:, q * 1024 : (q + 1) * 1024],
+                in0=sg[:],
+                scalar1=gabs[:, 0:1],
+                scalar2=None,
+                op0=ALU.mult,
+            )
+
+        def w_quant(h):
+            nc.vector.quantize_mx(
+                out=w_codes[:, h * 512 : (h + 1) * 512].bitcast(E4M3X4),
+                scales=w_scales[:, h * 512 : (h + 1) * 512],
+                in_=wg[:, h * 2048 : (h + 1) * 2048],
+            )
+
+        g_banks = {}
+        g_grouped = {}
+
+        def g_transposes(j):
+            g_banks[j] = transposes(g_words[2 * j], g_words[2 * j + 1], "gt%d" % j)
+
+        def g_copy(j):
+            gg = ring.tile([P, 1024], BF16, name="gg%d" % j, tag="gg", align_bytes=64)
+            nc.vector.tensor_copy(
+                out=gg[:].bitcast(F32).rearrange("p (m u) -> p m u", u=2),
+                in_=g_banks[j][:].rearrange("p (u m) -> p m u", u=2),
+            )
+            g_grouped[j] = gg
+
+        def g_quant(j):
+            nc.vector.quantize_mx(
+                out=g_codes[:, j * 256 : (j + 1) * 256].bitcast(E5M2X4),
+                scales=g_scales[:, j * 256 : (j + 1) * 256],
+                in_=g_grouped[j][:],
+            )
+
+        def products(j):
+            n = 0
+            for h in range(2):
+                for a in range(2):
+                    t = 2 * j + a
+                    acc = psum.tile([P, 512], F32, name="acc%d_%d" % (t, h), tag="bank")
+                    nc.tensor.matmul_mx(
+                        out=acc[:],
+                        lhsT=g_codes[:, t * P : (t + 1) * P].bitcast(E5M2X4),
+                        lhsT_scale=g_scales[:, t * P : (t + 1) * P],
+                        rhs=w_codes[:, h * 512 : (h + 1) * 512].bitcast(E4M3X4),
+                        rhs_scale=w_scales[:, h * 512 : (h + 1) * 512],
+                        start=True,
+                        stop=True,
+                    )
+                    dst = o_tiles[t][:, h * 512 : (h + 1) * 512]
+                    if n == 3:
+                        nc.vector.tensor_copy(out=dst, in_=acc[:])
+                    else:
+                        nc.scalar.copy(out=dst, in_=acc[:])
+                    n += 1
+
+        g_transposes(0)
+        g_transposes(1)
+        w_sign_mult(0)
+        w_sign_mult(1)
+        g_copy(0)
+        w_quant(0)
+        g_quant(0)
+        w_sign_mult(2)
+        w_sign_mult(3)
+        g_copy(1)
+        w_quant(1)
+
+        for j in range(PAIRS):
+            if j + 2 < PAIRS:
+                g_transposes(j + 2)
+                g_copy(j + 2)
+            if j + 1 < PAIRS:
+                g_quant(j + 1)
+            products(j)
+            last = 2 * j + 1
+            if last in store_of:
+                ot, first, width = store_of[last]
+                nc.sync.dma_start(
+                    out=out_view[:, first * K : (first + width) * K], in_=ot[:]
+                )

@@ -19,8 +19,9 @@ PAIRS = MT // 2
 FLOPS = 2 * M * K * N
 BYTES = K * N * 2 + 2 + M * N * 2 + M * K * 4
 
-G_CHUNKS = [2, 2, 4, 8, 8, 8]
-STORES = [2, 2, 4, 4, 4, 4, 4, 4, 4]
+G_CHUNKS = [2,2,4,8,16]
+STORES = [1,1,2,4,4,4,8,8]
+GAMMA_BY_PE = False
 
 
 def tile_binary_dense_t_kernel(tc, x, w, gamma, grad_out, out):
@@ -31,16 +32,23 @@ def tile_binary_dense_t_kernel(tc, x, w, gamma, grad_out, out):
         psum = ctx.enter_context(tc.psum_pool(name="psum", bufs=8))
         ctx.enter_context(tc.manual_schedule())
 
-        gam = keep.tile([P, 1], BF16, name="gam")
-        nc.scalar.dma_start(out=gam[:], in_=gamma.partition_broadcast(P))
+        if GAMMA_BY_PE:
+            grow = keep.tile([P, 32], BF16, name="grow")
+            nc.vector.memset(grow[:], 0.0)
+            ones = keep.tile([P, P], BF16, name="ones")
+            nc.vector.memset(ones[:], 1.0)
+            nc.scalar.dma_start(out=grow[0:1, 0:1], in_=gamma.rearrange("(o n) -> o n", o=1))
+        else:
+            gam = keep.tile([P, 1], BF16, name="gam")
+            nc.scalar.dma_start(out=gam[:], in_=gamma.partition_broadcast(P))
 
         w_view = w.rearrange("(i p) n -> p i n", p=P)
         w_raw = []
-        for h in range(2):
-            wr = keep.tile([P, 4 * N], BF16, name="w_raw%d" % h)
+        for q in range(4):
+            wr = keep.tile([P, 2 * N], BF16, name="w_raw%d" % q)
             nc.sync.dma_start(
-                out=wr[:].rearrange("p (i n) -> p i n", i=4),
-                in_=w_view[:, 4 * h : 4 * h + 4, :],
+                out=wr[:].rearrange("p (i n) -> p i n", i=2),
+                in_=w_view[:, 2 * q : 2 * q + 2, :],
             )
             w_raw.append(wr)
 
@@ -59,7 +67,6 @@ def tile_binary_dense_t_kernel(tc, x, w, gamma, grad_out, out):
         make_identity(nc, ident[:])
 
         gabs = keep.tile([P, 1], F32, name="gabs")
-        nc.scalar.activation(out=gabs[:], in_=gam[:], func=ACT.Abs)
 
         wg = keep.tile([P, 4 * K], BF16, name="wg", align_bytes=64)
         w_codes = keep.tile([P, K], U32, name="w_codes", align_bytes=64)
@@ -90,37 +97,35 @@ def tile_binary_dense_t_kernel(tc, x, w, gamma, grad_out, out):
             return bank
 
         w_banks = []
-        for h in range(2):
-            ww = w_raw[h][:].bitcast(F32)
-            for b in range(2):
-                w_banks.append(
-                    transposes(
-                        ww[:, (2 * b) * 256 : (2 * b + 1) * 256],
-                        ww[:, (2 * b + 1) * 256 : (2 * b + 2) * 256],
-                        "wt%d%d" % (h, b),
-                    )
-                )
+        w_signs = {}
 
-        def w_sign_mult(q):
+        def w_transposes(q):
+            ww = w_raw[q][:].bitcast(F32)
+            w_banks.append(transposes(ww[:, 0:256], ww[:, 256:512], "wt%d" % q))
+
+        def w_sign(q):
             sg = ring.tile([P, 1024], BF16, name="sg%d" % q, tag="sg")
             nc.scalar.activation(
                 out=sg[:].rearrange("p (k u e) -> p k u e", u=2, e=2),
                 in_=w_banks[q][:].bitcast(BF16).rearrange("p (u k e) -> p k u e", u=2, e=2),
                 func=ACT.Sign,
             )
+            w_signs[q] = sg
+
+        def w_mult(q):
             nc.vector.tensor_scalar(
                 out=wg[:, q * 1024 : (q + 1) * 1024],
-                in0=sg[:],
+                in0=w_signs[q][:],
                 scalar1=gabs[:, 0:1],
                 scalar2=None,
                 op0=ALU.mult,
             )
 
-        def w_quant(h):
+        def w_quant(q):
             nc.vector.quantize_mx(
-                out=w_codes[:, h * 512 : (h + 1) * 512].bitcast(E4M3X4),
-                scales=w_scales[:, h * 512 : (h + 1) * 512],
-                in_=wg[:, h * 2048 : (h + 1) * 2048],
+                out=w_codes[:, q * 256 : (q + 1) * 256].bitcast(E4M3X4),
+                scales=w_scales[:, q * 256 : (q + 1) * 256],
+                in_=wg[:, q * 1024 : (q + 1) * 1024],
             )
 
         g_banks = {}
@@ -144,8 +149,15 @@ def tile_binary_dense_t_kernel(tc, x, w, gamma, grad_out, out):
                 in_=g_grouped[j][:],
             )
 
+        def store_if_complete(t):
+            if t in store_of:
+                ot, first, width = store_of[t]
+                nc.sync.dma_start(
+                    out=out_view[:, first * K : (first + width) * K], in_=ot[:]
+                )
+
         def products(j):
-            n = 0
+            accs = []
             for h in range(2):
                 for a in range(2):
                     t = 2 * j + a
@@ -159,24 +171,43 @@ def tile_binary_dense_t_kernel(tc, x, w, gamma, grad_out, out):
                         start=True,
                         stop=True,
                     )
-                    dst = o_tiles[t][:, h * 512 : (h + 1) * 512]
-                    if n == 3:
-                        nc.vector.tensor_copy(out=dst, in_=acc[:])
-                    else:
-                        nc.scalar.copy(out=dst, in_=acc[:])
-                    n += 1
+                    accs.append((o_tiles[t][:, h * 512 : (h + 1) * 512], acc))
+            for n, (dst, acc) in enumerate(accs):
+                if n == 3:
+                    nc.vector.tensor_copy(out=dst, in_=acc[:])
+                else:
+                    nc.scalar.copy(out=dst, in_=acc[:])
+                if n >= 2:
+                    store_if_complete(2 * j + n - 2)
 
+        w_transposes(0)
+        w_transposes(1)
+        if GAMMA_BY_PE:
+            gps = psum.tile([P, 512], F32, name="gps", tag="bank")
+            nc.tensor.matmul(out=gps[:, 0:32], lhsT=ones[:], rhs=grow[:], start=True, stop=True)
+            w_sign(0)
+            nc.scalar.activation(out=gabs[:], in_=gps[:, 0:1], func=ACT.Abs)
+        else:
+            nc.scalar.activation(out=gabs[:], in_=gam[:], func=ACT.Abs)
+            w_sign(0)
+        w_transposes(2)
+        w_transposes(3)
         g_transposes(0)
         g_transposes(1)
-        w_sign_mult(0)
-        w_sign_mult(1)
-        g_copy(0)
+        w_mult(0)
         w_quant(0)
-        g_quant(0)
-        w_sign_mult(2)
-        w_sign_mult(3)
-        g_copy(1)
+        w_sign(1)
+        w_mult(1)
         w_quant(1)
+        g_copy(0)
+        w_sign(2)
+        w_mult(2)
+        g_quant(0)
+        w_quant(2)
+        w_sign(3)
+        w_mult(3)
+        w_quant(3)
+        g_copy(1)
 
         for j in range(PAIRS):
             if j + 2 < PAIRS:
@@ -185,9 +216,3 @@ def tile_binary_dense_t_kernel(tc, x, w, gamma, grad_out, out):
             if j + 1 < PAIRS:
                 g_quant(j + 1)
             products(j)
-            last = 2 * j + 1
-            if last in store_of:
-                ot, first, width = store_of[last]
-                nc.sync.dma_start(
-                    out=out_view[:, first * K : (first + width) * K], in_=ot[:]
-                )

@@ -19,9 +19,9 @@ PAIRS = MT // 2
 FLOPS = 2 * M * K * N
 BYTES = K * N * 2 + 2 + M * N * 2 + M * K * 4
 
-G_CHUNKS = [2,2,4,8,16]
-STORES = [1,1,2,4,4,4,8,8]
-GAMMA_BY_PE = False
+G_CHUNKS = [4,4,8,16]
+STORES = [1,1,2,4,4,4,4,4,4,4]
+VECTOR_BANKS = [[3]]
 
 
 def tile_binary_dense_t_kernel(tc, x, w, gamma, grad_out, out):
@@ -32,24 +32,14 @@ def tile_binary_dense_t_kernel(tc, x, w, gamma, grad_out, out):
         psum = ctx.enter_context(tc.psum_pool(name="psum", bufs=8))
         ctx.enter_context(tc.manual_schedule())
 
-        if GAMMA_BY_PE:
-            grow = keep.tile([P, 32], BF16, name="grow")
-            nc.vector.memset(grow[:], 0.0)
-            ones = keep.tile([P, P], BF16, name="ones")
-            nc.vector.memset(ones[:], 1.0)
-            nc.scalar.dma_start(out=grow[0:1, 0:1], in_=gamma.rearrange("(o n) -> o n", o=1))
-        else:
-            gam = keep.tile([P, 1], BF16, name="gam")
-            nc.scalar.dma_start(out=gam[:], in_=gamma.partition_broadcast(P))
+        gam = keep.tile([P, 1], BF16, name="gam")
+        nc.scalar.dma_start(out=gam[:], in_=gamma.partition_broadcast(P))
 
-        w_view = w.rearrange("(i p) n -> p i n", p=P)
+        w_view = w.rearrange("(h p i) n -> h p (i n)", h=2, i=4)
         w_raw = []
-        for q in range(4):
-            wr = keep.tile([P, 2 * N], BF16, name="w_raw%d" % q)
-            nc.sync.dma_start(
-                out=wr[:].rearrange("p (i n) -> p i n", i=2),
-                in_=w_view[:, 2 * q : 2 * q + 2, :],
-            )
+        for h in range(2):
+            wr = keep.tile([P, 4 * N], BF16, name="w_raw%d" % h)
+            nc.sync.dma_start(out=wr[:], in_=w_view[h])
             w_raw.append(wr)
 
         g_view = grad_out.rearrange("(p t) n -> p (t n)", t=MT)
@@ -66,7 +56,12 @@ def tile_binary_dense_t_kernel(tc, x, w, gamma, grad_out, out):
         ident = keep.tile([P, P], F32, name="ident")
         make_identity(nc, ident[:])
 
+        gf = keep.tile([P, 1], F32, name="gf")
         gabs = keep.tile([P, 1], F32, name="gabs")
+        nc.vector.tensor_copy(out=gf[:], in_=gam[:])
+        nc.vector.tensor_scalar(
+            out=gabs[:], in0=gf[:], scalar1=-1.0, scalar2=gf[:, 0:1], op0=ALU.mult, op1=ALU.max
+        )
 
         wg = keep.tile([P, 4 * K], BF16, name="wg", align_bytes=64)
         w_codes = keep.tile([P, K], U32, name="w_codes", align_bytes=64)
@@ -85,54 +80,60 @@ def tile_binary_dense_t_kernel(tc, x, w, gamma, grad_out, out):
             t0 += width
         out_view = out.rearrange("(p t) k -> p (t k)", t=MT)
 
-        def transposes(words_a, words_b, name):
-            bank = psum.tile([P, 512], F32, name=name, tag="bank")
-            for a, words in enumerate((words_a, words_b)):
-                for u in range(2):
-                    nc.tensor.transpose(
-                        bank[:, u * 256 + a * P : u * 256 + (a + 1) * P],
-                        words[:, u * P : (u + 1) * P],
-                        ident[:],
-                    )
-            return bank
-
-        w_banks = []
+        w_banks = {}
         w_signs = {}
 
         def w_transposes(q):
-            ww = w_raw[q][:].bitcast(F32)
-            w_banks.append(transposes(ww[:, 0:256], ww[:, 256:512], "wt%d" % q))
+            h, b = divmod(q, 2)
+            ww = w_raw[h][:].bitcast(F32)
+            bank = psum.tile([P, 512], F32, name="wt%d" % q, tag="bank")
+            for s in range(4):
+                nc.tensor.transpose(
+                    bank[:, s * P : (s + 1) * P],
+                    ww[:, (4 * b + s) * P : (4 * b + s + 1) * P],
+                    ident[:],
+                )
+            w_banks[q] = bank
 
         def w_sign(q):
             sg = ring.tile([P, 1024], BF16, name="sg%d" % q, tag="sg")
             nc.scalar.activation(
-                out=sg[:].rearrange("p (k u e) -> p k u e", u=2, e=2),
-                in_=w_banks[q][:].bitcast(BF16).rearrange("p (u k e) -> p k u e", u=2, e=2),
+                out=sg[:].rearrange("c (p s e) -> c p s e", s=4, e=2),
+                in_=w_banks[q][:].bitcast(BF16).rearrange("c (s p e) -> c p s e", s=4, e=2),
                 func=ACT.Sign,
             )
             w_signs[q] = sg
 
         def w_mult(q):
+            h, b = divmod(q, 2)
             nc.vector.tensor_scalar(
-                out=wg[:, q * 1024 : (q + 1) * 1024],
-                in0=w_signs[q][:],
+                out=wg[:, h * 2048 : (h + 1) * 2048].rearrange("c (p b r) -> c p b r", b=2, r=8)[:, :, b, :],
+                in0=w_signs[q][:].rearrange("c (p r) -> c p r", r=8),
                 scalar1=gabs[:, 0:1],
                 scalar2=None,
                 op0=ALU.mult,
             )
 
-        def w_quant(q):
+        def w_quant(h):
             nc.vector.quantize_mx(
-                out=w_codes[:, q * 256 : (q + 1) * 256].bitcast(E4M3X4),
-                scales=w_scales[:, q * 256 : (q + 1) * 256],
-                in_=wg[:, q * 1024 : (q + 1) * 1024],
+                out=w_codes[:, h * 512 : (h + 1) * 512].bitcast(E4M3X4),
+                scales=w_scales[:, h * 512 : (h + 1) * 512],
+                in_=wg[:, h * 2048 : (h + 1) * 2048],
             )
 
         g_banks = {}
         g_grouped = {}
 
         def g_transposes(j):
-            g_banks[j] = transposes(g_words[2 * j], g_words[2 * j + 1], "gt%d" % j)
+            bank = psum.tile([P, 512], F32, name="gt%d" % j, tag="bank")
+            for a in range(2):
+                for u in range(2):
+                    nc.tensor.transpose(
+                        bank[:, u * 256 + a * P : u * 256 + (a + 1) * P],
+                        g_words[2 * j + a][:, u * P : (u + 1) * P],
+                        ident[:],
+                    )
+            g_banks[j] = bank
 
         def g_copy(j):
             gg = ring.tile([P, 1024], BF16, name="gg%d" % j, tag="gg", align_bytes=64)
@@ -173,41 +174,30 @@ def tile_binary_dense_t_kernel(tc, x, w, gamma, grad_out, out):
                     )
                     accs.append((o_tiles[t][:, h * 512 : (h + 1) * 512], acc))
             for n, (dst, acc) in enumerate(accs):
-                if n == 3:
+                if n in VECTOR_BANKS[j % len(VECTOR_BANKS)]:
                     nc.vector.tensor_copy(out=dst, in_=acc[:])
                 else:
                     nc.scalar.copy(out=dst, in_=acc[:])
                 if n >= 2:
                     store_if_complete(2 * j + n - 2)
 
-        w_transposes(0)
-        w_transposes(1)
-        if GAMMA_BY_PE:
-            gps = psum.tile([P, 512], F32, name="gps", tag="bank")
-            nc.tensor.matmul(out=gps[:, 0:32], lhsT=ones[:], rhs=grow[:], start=True, stop=True)
-            w_sign(0)
-            nc.scalar.activation(out=gabs[:], in_=gps[:, 0:1], func=ACT.Abs)
-        else:
-            nc.scalar.activation(out=gabs[:], in_=gam[:], func=ACT.Abs)
-            w_sign(0)
-        w_transposes(2)
-        w_transposes(3)
+        for q in range(4):
+            w_transposes(q)
         g_transposes(0)
         g_transposes(1)
+        w_sign(0)
         w_mult(0)
-        w_quant(0)
         w_sign(1)
-        w_mult(1)
-        w_quant(1)
         g_copy(0)
+        w_mult(1)
+        w_quant(0)
         w_sign(2)
-        w_mult(2)
         g_quant(0)
-        w_quant(2)
+        w_mult(2)
+        g_copy(1)
         w_sign(3)
         w_mult(3)
-        w_quant(3)
-        g_copy(1)
+        w_quant(1)
 
         for j in range(PAIRS):
             if j + 2 < PAIRS:

@@ -20,7 +20,7 @@ FLOPS = 2 * M * K * N
 BYTES = K * N * 2 + 2 + M * N * 2 + M * K * 4
 
 G_CHUNKS = [4,4,8,16]
-STORES = [1,1,2,4,4,4,4,4,4,4]
+STORES = [1,1,2,2,2,4,4,4,4,4,4]
 VECTOR_BANKS = [[3]]
 
 
@@ -35,11 +35,11 @@ def tile_binary_dense_t_kernel(tc, x, w, gamma, grad_out, out):
         gam = keep.tile([P, 1], BF16, name="gam")
         nc.scalar.dma_start(out=gam[:], in_=gamma.partition_broadcast(P))
 
-        w_view = w.rearrange("(h p i) n -> h p (i n)", h=2, i=4)
+        w_view = w.rearrange("(q p d) n -> q p (d n)", q=4, d=2)
         w_raw = []
-        for h in range(2):
-            wr = keep.tile([P, 4 * N], BF16, name="w_raw%d" % h)
-            nc.sync.dma_start(out=wr[:], in_=w_view[h])
+        for q in range(4):
+            wr = keep.tile([P, 2 * N], BF16, name="w_raw%d" % q)
+            nc.sync.dma_start(out=wr[:], in_=w_view[q])
             w_raw.append(wr)
 
         g_view = grad_out.rearrange("(p t) n -> p (t n)", t=MT)
@@ -84,15 +84,10 @@ def tile_binary_dense_t_kernel(tc, x, w, gamma, grad_out, out):
         w_signs = {}
 
         def w_transposes(q):
-            h, b = divmod(q, 2)
-            ww = w_raw[h][:].bitcast(F32)
+            ww = w_raw[q][:].bitcast(F32)
             bank = psum.tile([P, 512], F32, name="wt%d" % q, tag="bank")
             for s in range(4):
-                nc.tensor.transpose(
-                    bank[:, s * P : (s + 1) * P],
-                    ww[:, (4 * b + s) * P : (4 * b + s + 1) * P],
-                    ident[:],
-                )
+                nc.tensor.transpose(bank[:, s * P : (s + 1) * P], ww[:, s * P : (s + 1) * P], ident[:])
             w_banks[q] = bank
 
         def w_sign(q):
@@ -105,20 +100,19 @@ def tile_binary_dense_t_kernel(tc, x, w, gamma, grad_out, out):
             w_signs[q] = sg
 
         def w_mult(q):
-            h, b = divmod(q, 2)
             nc.vector.tensor_scalar(
-                out=wg[:, h * 2048 : (h + 1) * 2048].rearrange("c (p b r) -> c p b r", b=2, r=8)[:, :, b, :],
-                in0=w_signs[q][:].rearrange("c (p r) -> c p r", r=8),
+                out=wg[:, q * 1024 : (q + 1) * 1024],
+                in0=w_signs[q][:],
                 scalar1=gabs[:, 0:1],
                 scalar2=None,
                 op0=ALU.mult,
             )
 
-        def w_quant(h):
+        def w_quant(q):
             nc.vector.quantize_mx(
-                out=w_codes[:, h * 512 : (h + 1) * 512].bitcast(E4M3X4),
-                scales=w_scales[:, h * 512 : (h + 1) * 512],
-                in_=wg[:, h * 2048 : (h + 1) * 2048],
+                out=w_codes[:, q * 256 : (q + 1) * 256].bitcast(E4M3X4),
+                scales=w_scales[:, q * 256 : (q + 1) * 256],
+                in_=wg[:, q * 1024 : (q + 1) * 1024],
             )
 
         g_banks = {}
@@ -188,16 +182,18 @@ def tile_binary_dense_t_kernel(tc, x, w, gamma, grad_out, out):
         w_sign(0)
         w_mult(0)
         w_sign(1)
-        g_copy(0)
-        w_mult(1)
         w_quant(0)
+        w_mult(1)
         w_sign(2)
-        g_quant(0)
-        w_mult(2)
-        g_copy(1)
-        w_sign(3)
-        w_mult(3)
+        g_copy(0)
         w_quant(1)
+        w_mult(2)
+        w_sign(3)
+        g_quant(0)
+        w_quant(2)
+        g_copy(1)
+        w_mult(3)
+        w_quant(3)
 
         for j in range(PAIRS):
             if j + 2 < PAIRS:

@@ -32,8 +32,11 @@ def tile_binary_dense_t_kernel(tc, x, w, gamma, grad_out, out):
         psum = ctx.enter_context(tc.psum_pool(name="psum", bufs=8))
         ctx.enter_context(tc.manual_schedule())
 
-        gam = keep.tile([P, 1], BF16, name="gam")
-        nc.scalar.dma_start(out=gam[:], in_=gamma.partition_broadcast(P))
+        gz = keep.tile([P, 2], BF16, name="gz")
+        nc.vector.memset(gz[:], 0.0)
+        nc.scalar.dma_start(out=gz[0:1, 0:1], in_=gamma.rearrange("(a b) -> a b", a=1))
+        ones = keep.tile([P, P], BF16, name="ones")
+        nc.vector.memset(ones[:], 1.0)
 
         w_view = w.rearrange("(q p d) n -> q p (d n)", q=4, d=2)
         w_raw = []
@@ -58,10 +61,14 @@ def tile_binary_dense_t_kernel(tc, x, w, gamma, grad_out, out):
 
         gf = keep.tile([P, 1], F32, name="gf")
         gabs = keep.tile([P, 1], F32, name="gabs")
-        nc.vector.tensor_copy(out=gf[:], in_=gam[:])
-        nc.vector.tensor_scalar(
-            out=gabs[:], in0=gf[:], scalar1=-1.0, scalar2=gf[:, 0:1], op0=ALU.mult, op1=ALU.max
-        )
+
+        def gamma_spread():
+            gm = psum.tile([P, 512], F32, name="gm", tag="bank")
+            nc.tensor.matmul(gm[:, 0:2], lhsT=ones[:], rhs=gz[:], start=True, stop=True)
+            nc.vector.tensor_copy(out=gf[:], in_=gm[:, 0:1])
+            nc.vector.tensor_scalar(
+                out=gabs[:], in0=gf[:], scalar1=-1.0, scalar2=gf[:, 0:1], op0=ALU.mult, op1=ALU.max
+            )
 
         wg = keep.tile([P, 4 * K], BF16, name="wg", align_bytes=64)
         w_codes = keep.tile([P, K], U32, name="w_codes", align_bytes=64)
@@ -175,7 +182,9 @@ def tile_binary_dense_t_kernel(tc, x, w, gamma, grad_out, out):
                 if n >= 2:
                     store_if_complete(2 * j + n - 2)
 
-        for q in range(4):
+        w_transposes(0)
+        gamma_spread()
+        for q in range(1, 4):
             w_transposes(q)
         g_transposes(0)
         g_transposes(1)

@@ -154,7 +154,8 @@ def tile_binary_dense_t_kernel(tc, x, w, gamma, grad_out, out):
         def store_if_complete(t):
             if t in store_of:
                 ot, first, width = store_of[t]
-                nc.sync.dma_start(
+                queue = nc.scalar if (width == 4 and (first // 4) % 2 == 1) else nc.sync
+                queue.dma_start(
                     out=out_view[:, first * K : (first + width) * K], in_=ot[:]
                 )
 

@@ -136,9 +136,10 @@ def tile_binary_dense_t_kernel(tc, x, w, gamma, grad_out, out):
                     )
             g_banks[j] = bank
 
-        def g_copy(j):
+        def g_copy(j, on_scalar=False):
             gg = ring.tile([P, 1024], BF16, name="gg%d" % j, tag="gg", align_bytes=64)
-            nc.vector.tensor_copy(
+            copy = nc.scalar.copy if on_scalar else nc.vector.tensor_copy
+            copy(
                 out=gg[:].bitcast(F32).rearrange("p (m u) -> p m u", u=2),
                 in_=g_banks[j][:].rearrange("p (u m) -> p m u", u=2),
             )
@@ -199,14 +200,16 @@ def tile_binary_dense_t_kernel(tc, x, w, gamma, grad_out, out):
         w_quant(1)
         w_mult(2)
         w_sign(3)
+        g_copy(1, on_scalar=True)
+        g_transposes(2)
+        g_copy(2, on_scalar=True)
         g_quant(0)
         w_quant(2)
-        g_copy(1)
         w_mult(3)
         w_quant(3)
 
         for j in range(PAIRS):
-            if j + 2 < PAIRS:
+            if 0 < j and j + 2 < PAIRS:
                 g_transposes(j + 2)
                 g_copy(j + 2)
             if j + 1 < PAIRS:

from contextlib import ExitStack

import concourse.mybir as mybir
from concourse.masks import make_identity

F32 = mybir.dt.float32
BF16 = mybir.dt.bfloat16
U32 = mybir.dt.uint32
U8 = mybir.dt.uint8
E4M3X4 = mybir.dt.float8_e4m3fn_x4
E5M2X4 = mybir.dt.float8_e5m2_x4
ACT = mybir.ActivationFunctionType
ALU = mybir.AluOpType

P = 128
M, K, N = 4096, 1024, 512
MT = M // P
PAIRS = MT // 2
FLOPS = 2 * M * K * N
BYTES = K * N * 2 + 2 + M * N * 2 + M * K * 4

G_CHUNKS = [4,4,8,16]
STORES = [1,1,2,2,2,4,4,4,4,4,4]
VECTOR_BANKS = [[3]]


def tile_binary_dense_t_kernel(tc, x, w, gamma, grad_out, out):
    nc = tc.nc
    with ExitStack() as ctx:
        keep = ctx.enter_context(tc.tile_pool(name="keep", bufs=1))
        ring = ctx.enter_context(tc.tile_pool(name="ring", bufs=3))
        psum = ctx.enter_context(tc.psum_pool(name="psum", bufs=8))
        ctx.enter_context(tc.manual_schedule())

        gz = keep.tile([P, 2], BF16, name="gz")
        nc.vector.memset(gz[:], 0.0)
        nc.scalar.dma_start(out=gz[0:1, 0:1], in_=gamma.rearrange("(a b) -> a b", a=1))
        ones = keep.tile([P, P], BF16, name="ones")
        nc.vector.memset(ones[:], 1.0)

        w_view = w.rearrange("(q p d) n -> q p (d n)", q=4, d=2)
        w_raw = []
        for q in range(4):
            wr = keep.tile([P, 2 * N], BF16, name="w_raw%d" % q)
            nc.sync.dma_start(out=wr[:], in_=w_view[q])
            w_raw.append(wr)

        g_view = grad_out.rearrange("(p t) n -> p (t n)", t=MT)
        g_words = {}
        t0 = 0
        for c, width in enumerate(G_CHUNKS):
            gr = keep.tile([P, width * N], BF16, name="g_raw%d" % c)
            nc.sync.dma_start(out=gr[:], in_=g_view[:, t0 * N : (t0 + width) * N])
            gw = gr[:].bitcast(F32)
            for a in range(width):
                g_words[t0 + a] = gw[:, a * 256 : (a + 1) * 256]
            t0 += width

        ident = keep.tile([P, P], F32, name="ident")
        make_identity(nc, ident[:])

        gf = keep.tile([P, 1], F32, name="gf")
        gabs = keep.tile([P, 1], F32, name="gabs")

        def gamma_spread():
            gm = psum.tile([P, 512], F32, name="gm", tag="bank")
            nc.tensor.matmul(gm[:, 0:2], lhsT=ones[:], rhs=gz[:], start=True, stop=True)
            nc.vector.tensor_copy(out=gf[:], in_=gm[:, 0:1])
            nc.vector.tensor_scalar(
                out=gabs[:], in0=gf[:], scalar1=-1.0, scalar2=gf[:, 0:1], op0=ALU.mult, op1=ALU.max
            )

        wg = keep.tile([P, 4 * K], BF16, name="wg", align_bytes=64)
        w_codes = keep.tile([P, K], U32, name="w_codes", align_bytes=64)
        w_scales = keep.tile([P, K], U8, name="w_scales", align_bytes=64)
        g_codes = keep.tile([P, M], U32, name="g_codes", align_bytes=64)
        g_scales = keep.tile([P, M], U8, name="g_scales", align_bytes=64)

        o_tiles = {}
        store_of = {}
        t0 = 0
        for s, width in enumerate(STORES):
            ot = keep.tile([P, width * K], F32, name="o%d" % s)
            for a in range(width):
                o_tiles[t0 + a] = ot[:, a * K : (a + 1) * K]
            store_of[t0 + width - 1] = (ot, t0, width)
            t0 += width
        out_view = out.rearrange("(p t) k -> p (t k)", t=MT)

        w_banks = {}
        w_signs = {}

        def w_transposes(q):
            ww = w_raw[q][:].bitcast(F32)
            bank = psum.tile([P, 512], F32, name="wt%d" % q, tag="bank")
            for s in range(4):
                nc.tensor.transpose(bank[:, s * P : (s + 1) * P], ww[:, s * P : (s + 1) * P], ident[:])
            w_banks[q] = bank

        def w_sign(q):
            sg = ring.tile([P, 1024], BF16, name="sg%d" % q, tag="sg")
            nc.scalar.activation(
                out=sg[:].rearrange("c (p s e) -> c p s e", s=4, e=2),
                in_=w_banks[q][:].bitcast(BF16).rearrange("c (s p e) -> c p s e", s=4, e=2),
                func=ACT.Sign,
            )
            w_signs[q] = sg

        def w_mult(q):
            nc.vector.tensor_scalar(
                out=wg[:, q * 1024 : (q + 1) * 1024],
                in0=w_signs[q][:],
                scalar1=gabs[:, 0:1],
                scalar2=None,
                op0=ALU.mult,
            )

        def w_quant(q):
            nc.vector.quantize_mx(
                out=w_codes[:, q * 256 : (q + 1) * 256].bitcast(E4M3X4),
                scales=w_scales[:, q * 256 : (q + 1) * 256],
                in_=wg[:, q * 1024 : (q + 1) * 1024],
            )

        g_banks = {}
        g_grouped = {}

        def g_transposes(j):
            bank = psum.tile([P, 512], F32, name="gt%d" % j, tag="bank")
            for a in range(2):
                for u in range(2):
                    nc.tensor.transpose(
                        bank[:, u * 256 + a * P : u * 256 + (a + 1) * P],
                        g_words[2 * j + a][:, u * P : (u + 1) * P],
                        ident[:],
                    )
            g_banks[j] = bank

        def g_copy(j, on_scalar=False):
            gg = ring.tile([P, 1024], BF16, name="gg%d" % j, tag="gg", align_bytes=64)
            copy = nc.scalar.copy if on_scalar else nc.vector.tensor_copy
            copy(
                out=gg[:].bitcast(F32).rearrange("p (m u) -> p m u", u=2),
                in_=g_banks[j][:].rearrange("p (u m) -> p m u", u=2),
            )
            g_grouped[j] = gg

        def g_quant(j):
            nc.vector.quantize_mx(
                out=g_codes[:, j * 256 : (j + 1) * 256].bitcast(E5M2X4),
                scales=g_scales[:, j * 256 : (j + 1) * 256],
                in_=g_grouped[j][:],
            )

        def store_if_complete(t):
            if t in store_of:
                ot, first, width = store_of[t]
                queue = nc.scalar if (width == 4 and (first // 4) % 2 == 1) else nc.sync
                queue.dma_start(
                    out=out_view[:, first * K : (first + width) * K], in_=ot[:]
                )

        def products(j):
            accs = []
            for h in range(2):
                for a in range(2):
                    t = 2 * j + a
                    acc = psum.tile([P, 512], F32, name="acc%d_%d" % (t, h), tag="bank")
                    nc.tensor.matmul_mx(
                        out=acc[:],
                        lhsT=g_codes[:, t * P : (t + 1) * P].bitcast(E5M2X4),
                        lhsT_scale=g_scales[:, t * P : (t + 1) * P],
                        rhs=w_codes[:, h * 512 : (h + 1) * 512].bitcast(E4M3X4),
                        rhs_scale=w_scales[:, h * 512 : (h + 1) * 512],
                        start=True,
                        stop=True,
                    )
                    accs.append((o_tiles[t][:, h * 512 : (h + 1) * 512], acc))
            for n, (dst, acc) in enumerate(accs):
                if n in VECTOR_BANKS[j % len(VECTOR_BANKS)]:
                    nc.vector.tensor_copy(out=dst, in_=acc[:])
                else:
                    nc.scalar.copy(out=dst, in_=acc[:])
                if n >= 2:
                    store_if_complete(2 * j + n - 2)

        w_transposes(0)
        gamma_spread()
        for q in range(1, 4):
            w_transposes(q)
        g_transposes(0)
        g_transposes(1)
        w_sign(0)
        w_mult(0)
        w_sign(1)
        w_quant(0)
        w_mult(1)
        w_sign(2)
        g_copy(0)
        w_quant(1)
        w_mult(2)
        w_sign(3)
        g_copy(1, on_scalar=True)
        g_transposes(2)
        g_copy(2, on_scalar=True)
        g_quant(0)
        w_quant(2)
        w_mult(3)
        w_quant(3)

        for j in range(PAIRS):
            if 0 < j and j + 2 < PAIRS:
                g_transposes(j + 2)
                g_copy(j + 2)
            if j + 1 < PAIRS:
                g_quant(j + 1)
            products(j)
